import numpy as np
import ml_dtypes

BF16 = ml_dtypes.bfloat16


def bf(x):
    return np.asarray(x, np.float32).astype(BF16)


def f32(x):
    return np.asarray(x, np.float32)


def f64(x):
    return np.asarray(x).astype(np.float64)


def striped(idx):
    return np.tile(idx.reshape(-1, 16).T, (8, 1))


C, S, N, M = 1024, 1024, 512, 128


def silu(v):
    return v / (1.0 + np.exp(-v))


def setup_inputs():
    return {"x": f32(np.random.standard_normal((C, S))), "hv": f32(np.random.standard_normal((C, N))), "wd": bf(np.random.standard_normal((C, M)) / np.sqrt(2.0 * C)), "wp": bf(np.random.standard_normal((C, M)) / np.sqrt(2.0 * C)), "ws": f32(0.5 * np.random.standard_normal((M, 1))), "wf": f32(0.5 * np.random.standard_normal((M, 1))), "b1": f32(0.1 * np.random.standard_normal((M, 1))), "se": f32(np.random.uniform(size=(1, N))), "fe": f32(np.random.uniform(size=(1, N))), "offs": striped(np.random.permutation(np.tile(np.arange(S), 2))[:N])}


def reference(x, hv, wd, wp, ws, wf, b1, se, fe, offs):
    idx = offs[:16].T.reshape(-1)
    xu = f64(x)[:, idx]
    diff = np.abs(xu + (-f64(hv)))
    prod = xu * f64(hv)
    pre = f64(wd).T @ diff + f64(wp).T @ prod + f64(ws) * f64(se) + f64(wf) * f64(fe) + f64(b1)
    return silu(pre)

@@ -1,0 +1,75 @@
+import concourse.mybir as mybir
+
+F32 = mybir.dt.float32
+BF16 = mybir.dt.bfloat16
+U16 = mybir.dt.uint16
+ACT = mybir.ActivationFunctionType
+ALU = mybir.AluOpType
+
+P = 128
+C, S, N, M = 1024, 1024, 512, 128
+BLOCKS = C // P
+EDGE_ROWS = 3
+
+FLOPS = 2 * (2 * C + EDGE_ROWS) * M * N
+
+
+def tile_edgegate_kernel(tc, x, hv, wd, wp, ws, wf, b1, se, fe, offs, out):
+    nc = tc.nc
+    with (
+        tc.tile_pool(name="held", bufs=1) as held,
+        tc.tile_pool(name="blocks", bufs=BLOCKS) as blocks,
+        tc.psum_pool(name="psum", bufs=1) as psum,
+    ):
+        offsets = held.tile([P, N // 16], U16, name="offsets")
+        nc.sync.dma_start(offsets[:], offs)
+
+        edge_weights = held.tile([EDGE_ROWS, M], F32, name="edge_weights")
+        edge_features = held.tile([EDGE_ROWS, N], F32, name="edge_features")
+        nc.vector.memset(edge_features[0:1, :], 1.0)
+        nc.scalar.dma_start(edge_weights[0:1, :], b1.rearrange("m o -> o m"))
+        nc.scalar.dma_start(edge_weights[1:2, :], ws.rearrange("m o -> o m"))
+        nc.scalar.dma_start(edge_weights[2:3, :], wf.rearrange("m o -> o m"))
+        nc.scalar.dma_start(edge_features[1:2, :], se)
+        nc.scalar.dma_start(edge_features[2:3, :], fe)
+
+        wd_sb = held.tile([P, BLOCKS, M], BF16, name="wd_sb")
+        wp_sb = held.tile([P, BLOCKS, M], BF16, name="wp_sb")
+        x_blocks = []
+        hv_blocks = []
+        for k in range(BLOCKS):
+            x_blk = blocks.tile([P, S], F32, name="x_blk")
+            hv_blk = blocks.tile([P, N], F32, name="hv_blk")
+            nc.sync.dma_start(x_blk[:], x[k * P : (k + 1) * P, :])
+            nc.sync.dma_start(hv_blk[:], hv[k * P : (k + 1) * P, :])
+            x_blocks.append(x_blk)
+            hv_blocks.append(hv_blk)
+            if k == 1:
+                nc.sync.dma_start(wp_sb[:], wp.rearrange("(k p) m -> p k m", p=P))
+                nc.sync.dma_start(wd_sb[:], wd.rearrange("(k p) m -> p k m", p=P))
+
+        pre = psum.tile([M, N], F32, name="pre")
+        nc.tensor.matmul(pre[:], edge_weights[:], edge_features[:], start=True, stop=False)
+
+        for k in range(BLOCKS):
+            looked_up = x_blocks[k][:].indirect(offsets[:])
+
+            neg_hv = blocks.tile([P, N], F32, name="neg_hv")
+            nc.scalar.activation(neg_hv[:], hv_blocks[k][:], ACT.Copy, scale=-1.0)
+
+            prod = blocks.tile([P, N], F32, name="prod")
+            nc.vector.tensor_tensor(prod[:], looked_up, hv_blocks[k][:], ALU.mult)
+            signed_diff = blocks.tile([P, N], F32, name="signed_diff")
+            nc.vector.tensor_tensor(signed_diff[:], looked_up, neg_hv[:], ALU.add)
+
+            prod_bf = blocks.tile([P, N], BF16, name="prod_bf")
+            nc.scalar.activation(prod_bf[:], prod[:], ACT.Copy)
+            diff_bf = blocks.tile([P, N], BF16, name="diff_bf")
+            nc.scalar.activation(diff_bf[:], signed_diff[:], ACT.Abs)
+
+            nc.tensor.matmul(pre[:], wp_sb[:, k, :], prod_bf[:], start=False, stop=False)
+            nc.tensor.matmul(pre[:], wd_sb[:, k, :], diff_bf[:], start=False, stop=(k == BLOCKS - 1))
+
+        gate = held.tile([M, N], F32, name="gate")
+        nc.scalar.activation(gate[:], pre[:], ACT.Silu)
+        nc.sync.dma_start(out, gate[:])

@@ -27,11 +27,14 @@ def tile_edgegate_kernel(tc, x, hv, wd, wp, ws, wf, b1, se, fe, offs, out):
         edge_weights = held.tile([EDGE_ROWS, M], F32, name="edge_weights")
         edge_features = held.tile([EDGE_ROWS, N], F32, name="edge_features")
         nc.vector.memset(edge_features[0:1, :], 1.0)
-        nc.scalar.dma_start(edge_weights[0:1, :], b1.rearrange("m o -> o m"))
-        nc.scalar.dma_start(edge_weights[1:2, :], ws.rearrange("m o -> o m"))
-        nc.scalar.dma_start(edge_weights[2:3, :], wf.rearrange("m o -> o m"))
-        nc.scalar.dma_start(edge_features[1:2, :], se)
-        nc.scalar.dma_start(edge_features[2:3, :], fe)
+        nc.gpsimd.dma_start(edge_weights[0:1, :], b1.rearrange("m o -> o m"))
+        nc.gpsimd.dma_start(edge_weights[1:2, :], ws.rearrange("m o -> o m"))
+        nc.gpsimd.dma_start(edge_weights[2:3, :], wf.rearrange("m o -> o m"))
+        nc.gpsimd.dma_start(edge_features[1:2, :], se)
+        nc.gpsimd.dma_start(edge_features[2:3, :], fe)
+
+        warm = held.tile([1, 1], F32, name="warm")
+        nc.scalar.activation(warm[:], edge_features[0:1, 0:1], ACT.Silu)
 
         wd_sb = held.tile([P, BLOCKS, M], BF16, name="wd_sb")
         wp_sb = held.tile([P, BLOCKS, M], BF16, name="wp_sb")
@@ -40,13 +43,13 @@ def tile_edgegate_kernel(tc, x, hv, wd, wp, ws, wf, b1, se, fe, offs, out):
         for k in range(BLOCKS):
             x_blk = blocks.tile([P, S], F32, name="x_blk")
             hv_blk = blocks.tile([P, N], F32, name="hv_blk")
-            nc.sync.dma_start(x_blk[:], x[k * P : (k + 1) * P, :])
             nc.sync.dma_start(hv_blk[:], hv[k * P : (k + 1) * P, :])
+            nc.sync.dma_start(x_blk[:], x[k * P : (k + 1) * P, :])
             x_blocks.append(x_blk)
             hv_blocks.append(hv_blk)
             if k == 1:
-                nc.sync.dma_start(wp_sb[:], wp.rearrange("(k p) m -> p k m", p=P))
                 nc.sync.dma_start(wd_sb[:], wd.rearrange("(k p) m -> p k m", p=P))
+                nc.sync.dma_start(wp_sb[:], wp.rearrange("(k p) m -> p k m", p=P))
 
         pre = psum.tile([M, N], F32, name="pre")
         nc.tensor.matmul(pre[:], edge_weights[:], edge_features[:], start=True, stop=False)
@@ -57,18 +60,18 @@ def tile_edgegate_kernel(tc, x, hv, wd, wp, ws, wf, b1, se, fe, offs, out):
             neg_hv = blocks.tile([P, N], F32, name="neg_hv")
             nc.scalar.activation(neg_hv[:], hv_blocks[k][:], ACT.Copy, scale=-1.0)
 
-            prod = blocks.tile([P, N], F32, name="prod")
-            nc.vector.tensor_tensor(prod[:], looked_up, hv_blocks[k][:], ALU.mult)
             signed_diff = blocks.tile([P, N], F32, name="signed_diff")
             nc.vector.tensor_tensor(signed_diff[:], looked_up, neg_hv[:], ALU.add)
+            prod = blocks.tile([P, N], F32, name="prod")
+            nc.vector.tensor_tensor(prod[:], looked_up, hv_blocks[k][:], ALU.mult)
 
-            prod_bf = blocks.tile([P, N], BF16, name="prod_bf")
-            nc.scalar.activation(prod_bf[:], prod[:], ACT.Copy)
             diff_bf = blocks.tile([P, N], BF16, name="diff_bf")
             nc.scalar.activation(diff_bf[:], signed_diff[:], ACT.Abs)
+            prod_bf = blocks.tile([P, N], BF16, name="prod_bf")
+            nc.scalar.activation(prod_bf[:], prod[:], ACT.Copy)
 
-            nc.tensor.matmul(pre[:], wp_sb[:, k, :], prod_bf[:], start=False, stop=False)
-            nc.tensor.matmul(pre[:], wd_sb[:, k, :], diff_bf[:], start=False, stop=(k == BLOCKS - 1))
+            nc.tensor.matmul(pre[:], wd_sb[:, k, :], diff_bf[:], start=False, stop=False)
+            nc.tensor.matmul(pre[:], wp_sb[:, k, :], prod_bf[:], start=False, stop=(k == BLOCKS - 1))
 
         gate = held.tile([M, N], F32, name="gate")
         nc.scalar.activation(gate[:], pre[:], ACT.Silu)

@@ -10,6 +10,7 @@ P = 128
 C, S, N, M = 1024, 1024, 512, 128
 BLOCKS = C // P
 EDGE_ROWS = 3
+HALVES = (slice(0, N // 2), slice(N // 2, N))
 
 FLOPS = 2 * (2 * C + EDGE_ROWS) * M * N
 
@@ -27,11 +28,6 @@ def tile_edgegate_kernel(tc, x, hv, wd, wp, ws, wf, b1, se, fe, offs, out):
         edge_weights = held.tile([EDGE_ROWS, M], F32, name="edge_weights")
         edge_features = held.tile([EDGE_ROWS, N], F32, name="edge_features")
         nc.vector.memset(edge_features[0:1, :], 1.0)
-        nc.gpsimd.dma_start(edge_weights[0:1, :], b1.rearrange("m o -> o m"))
-        nc.gpsimd.dma_start(edge_weights[1:2, :], ws.rearrange("m o -> o m"))
-        nc.gpsimd.dma_start(edge_weights[2:3, :], wf.rearrange("m o -> o m"))
-        nc.gpsimd.dma_start(edge_features[1:2, :], se)
-        nc.gpsimd.dma_start(edge_features[2:3, :], fe)
 
         warm = held.tile([1, 1], F32, name="warm")
         nc.scalar.activation(warm[:], edge_features[0:1, 0:1], ACT.Silu)
@@ -47,14 +43,22 @@ def tile_edgegate_kernel(tc, x, hv, wd, wp, ws, wf, b1, se, fe, offs, out):
             nc.sync.dma_start(x_blk[:], x[k * P : (k + 1) * P, :])
             x_blocks.append(x_blk)
             hv_blocks.append(hv_blk)
+            if k == 0:
+                nc.sync.dma_start(edge_weights[0:1, :], b1.rearrange("m o -> o m"))
+                nc.sync.dma_start(edge_weights[1:2, :], ws.rearrange("m o -> o m"))
+                nc.sync.dma_start(edge_weights[2:3, :], wf.rearrange("m o -> o m"))
+                nc.sync.dma_start(edge_features[1:2, :], se)
+                nc.sync.dma_start(edge_features[2:3, :], fe)
             if k == 1:
                 nc.sync.dma_start(wd_sb[:], wd.rearrange("(k p) m -> p k m", p=P))
                 nc.sync.dma_start(wp_sb[:], wp.rearrange("(k p) m -> p k m", p=P))
 
-        pre = psum.tile([M, N], F32, name="pre")
-        nc.tensor.matmul(pre[:], edge_weights[:], edge_features[:], start=True, stop=False)
+        pre = [psum.tile([M, N // 2], F32, name=f"pre{h}") for h in range(len(HALVES))]
+        for h, cols in enumerate(HALVES):
+            nc.tensor.matmul(pre[h][:], edge_weights[:], edge_features[:, cols], start=True, stop=False)
 
         for k in range(BLOCKS):
+            last = k == BLOCKS - 1
             looked_up = x_blocks[k][:].indirect(offsets[:])
 
             neg_hv = blocks.tile([P, N], F32, name="neg_hv")
@@ -68,11 +72,19 @@ def tile_edgegate_kernel(tc, x, hv, wd, wp, ws, wf, b1, se, fe, offs, out):
             diff_bf = blocks.tile([P, N], BF16, name="diff_bf")
             nc.scalar.activation(diff_bf[:], signed_diff[:], ACT.Abs)
             prod_bf = blocks.tile([P, N], BF16, name="prod_bf")
-            nc.scalar.activation(prod_bf[:], prod[:], ACT.Copy)
+            if last:
+                nc.scalar.activation(prod_bf[:, HALVES[0]], prod[:, HALVES[0]], ACT.Copy)
+                nc.vector.tensor_copy(prod_bf[:, HALVES[1]], prod[:, HALVES[1]])
+            else:
+                nc.scalar.activation(prod_bf[:], prod[:], ACT.Copy)
 
-            nc.tensor.matmul(pre[:], wd_sb[:, k, :], diff_bf[:], start=False, stop=False)
-            nc.tensor.matmul(pre[:], wp_sb[:, k, :], prod_bf[:], start=False, stop=(k == BLOCKS - 1))
+            for h, cols in enumerate(HALVES):
+                nc.tensor.matmul(pre[h][:], wd_sb[:, k, :], diff_bf[:, cols], start=False, stop=False)
+            for h, cols in enumerate(HALVES):
+                nc.tensor.matmul(pre[h][:], wp_sb[:, k, :], prod_bf[:, cols], start=False, stop=last)
 
-        gate = held.tile([M, N], F32, name="gate")
-        nc.scalar.activation(gate[:], pre[:], ACT.Silu)
-        nc.sync.dma_start(out, gate[:])
+        for h, cols in enumerate(HALVES):
+            gate = held.tile([M, N // 2], F32, name=f"gate{h}")
+            nc.scalar.activation(gate[:], pre[h][:], ACT.Silu)
+            queue = nc.sync if h == 0 else nc.scalar
+            queue.dma_start(out[:, cols], gate[:])

@@ -28,10 +28,17 @@ def tile_edgegate_kernel(tc, x, hv, wd, wp, ws, wf, b1, se, fe, offs, out):
         edge_weights = held.tile([EDGE_ROWS, M], F32, name="edge_weights")
         edge_features = held.tile([EDGE_ROWS, N], F32, name="edge_features")
         nc.vector.memset(edge_features[0:1, :], 1.0)
+        nc.gpsimd.dma_start(edge_weights[0:1, :], b1.rearrange("m o -> o m"))
+        nc.gpsimd.dma_start(edge_weights[1:2, :], ws.rearrange("m o -> o m"))
+        nc.gpsimd.dma_start(edge_weights[2:3, :], wf.rearrange("m o -> o m"))
+        nc.gpsimd.dma_start(edge_features[1:2, :], se)
+        nc.gpsimd.dma_start(edge_features[2:3, :], fe)
 
         warm = held.tile([1, 1], F32, name="warm")
         nc.scalar.activation(warm[:], edge_features[0:1, 0:1], ACT.Silu)
 
+        x_by_block = x.rearrange("(p k) s -> k p s", k=BLOCKS)
+        hv_by_block = hv.rearrange("(p k) n -> k p n", k=BLOCKS)
         wd_sb = held.tile([P, BLOCKS, M], BF16, name="wd_sb")
         wp_sb = held.tile([P, BLOCKS, M], BF16, name="wp_sb")
         x_blocks = []
@@ -39,26 +46,18 @@ def tile_edgegate_kernel(tc, x, hv, wd, wp, ws, wf, b1, se, fe, offs, out):
         for k in range(BLOCKS):
             x_blk = blocks.tile([P, S], F32, name="x_blk")
             hv_blk = blocks.tile([P, N], F32, name="hv_blk")
-            nc.sync.dma_start(hv_blk[:], hv[k * P : (k + 1) * P, :])
-            nc.sync.dma_start(x_blk[:], x[k * P : (k + 1) * P, :])
+            nc.sync.dma_start(hv_blk[:], hv_by_block[k])
+            nc.sync.dma_start(x_blk[:], x_by_block[k])
             x_blocks.append(x_blk)
             hv_blocks.append(hv_blk)
-            if k == 0:
-                nc.sync.dma_start(edge_weights[0:1, :], b1.rearrange("m o -> o m"))
-                nc.sync.dma_start(edge_weights[1:2, :], ws.rearrange("m o -> o m"))
-                nc.sync.dma_start(edge_weights[2:3, :], wf.rearrange("m o -> o m"))
-                nc.sync.dma_start(edge_features[1:2, :], se)
-                nc.sync.dma_start(edge_features[2:3, :], fe)
             if k == 1:
-                nc.sync.dma_start(wd_sb[:], wd.rearrange("(k p) m -> p k m", p=P))
-                nc.sync.dma_start(wp_sb[:], wp.rearrange("(k p) m -> p k m", p=P))
+                nc.sync.dma_start(wd_sb[:], wd.rearrange("(p k) m -> p k m", k=BLOCKS))
+                nc.sync.dma_start(wp_sb[:], wp.rearrange("(p k) m -> p k m", k=BLOCKS))
 
         pre = [psum.tile([M, N // 2], F32, name=f"pre{h}") for h in range(len(HALVES))]
-        for h, cols in enumerate(HALVES):
-            nc.tensor.matmul(pre[h][:], edge_weights[:], edge_features[:, cols], start=True, stop=False)
 
         for k in range(BLOCKS):
-            last = k == BLOCKS - 1
+            first, last = k == 0, k == BLOCKS - 1
             looked_up = x_blocks[k][:].indirect(offsets[:])
 
             neg_hv = blocks.tile([P, N], F32, name="neg_hv")
@@ -78,8 +77,11 @@ def tile_edgegate_kernel(tc, x, hv, wd, wp, ws, wf, b1, se, fe, offs, out):
             else:
                 nc.scalar.activation(prod_bf[:], prod[:], ACT.Copy)
 
+            if last:
+                for h, cols in enumerate(HALVES):
+                    nc.tensor.matmul(pre[h][:], edge_weights[:], edge_features[:, cols], start=False, stop=False)
             for h, cols in enumerate(HALVES):
-                nc.tensor.matmul(pre[h][:], wd_sb[:, k, :], diff_bf[:, cols], start=False, stop=False)
+                nc.tensor.matmul(pre[h][:], wd_sb[:, k, :], diff_bf[:, cols], start=first, stop=False)
             for h, cols in enumerate(HALVES):
                 nc.tensor.matmul(pre[h][:], wp_sb[:, k, :], prod_bf[:, cols], start=False, stop=last)
 

@@ -77,7 +77,7 @@ def tile_edgegate_kernel(tc, x, hv, wd, wp, ws, wf, b1, se, fe, offs, out):
             else:
                 nc.scalar.activation(prod_bf[:], prod[:], ACT.Copy)
 
-            if last:
+            if k == BLOCKS // 2:
                 for h, cols in enumerate(HALVES):
                     nc.tensor.matmul(pre[h][:], edge_weights[:], edge_features[:, cols], start=False, stop=False)
             for h, cols in enumerate(HALVES):

@@ -63,27 +63,27 @@ def tile_edgegate_kernel(tc, x, hv, wd, wp, ws, wf, b1, se, fe, offs, out):
             neg_hv = blocks.tile([P, N], F32, name="neg_hv")
             nc.scalar.activation(neg_hv[:], hv_blocks[k][:], ACT.Copy, scale=-1.0)
 
-            signed_diff = blocks.tile([P, N], F32, name="signed_diff")
-            nc.vector.tensor_tensor(signed_diff[:], looked_up, neg_hv[:], ALU.add)
             prod = blocks.tile([P, N], F32, name="prod")
             nc.vector.tensor_tensor(prod[:], looked_up, hv_blocks[k][:], ALU.mult)
+            signed_diff = blocks.tile([P, N], F32, name="signed_diff")
+            nc.vector.tensor_tensor(signed_diff[:], looked_up, neg_hv[:], ALU.add)
 
-            diff_bf = blocks.tile([P, N], BF16, name="diff_bf")
-            nc.scalar.activation(diff_bf[:], signed_diff[:], ACT.Abs)
             prod_bf = blocks.tile([P, N], BF16, name="prod_bf")
+            nc.scalar.activation(prod_bf[:], prod[:], ACT.Copy)
+            diff_bf = blocks.tile([P, N], BF16, name="diff_bf")
             if last:
-                nc.scalar.activation(prod_bf[:, HALVES[0]], prod[:, HALVES[0]], ACT.Copy)
-                nc.vector.tensor_copy(prod_bf[:, HALVES[1]], prod[:, HALVES[1]])
+                for cols in HALVES:
+                    nc.scalar.activation(diff_bf[:, cols], signed_diff[:, cols], ACT.Abs)
             else:
-                nc.scalar.activation(prod_bf[:], prod[:], ACT.Copy)
+                nc.scalar.activation(diff_bf[:], signed_diff[:], ACT.Abs)
 
             if k == BLOCKS // 2:
                 for h, cols in enumerate(HALVES):
                     nc.tensor.matmul(pre[h][:], edge_weights[:], edge_features[:, cols], start=False, stop=False)
             for h, cols in enumerate(HALVES):
-                nc.tensor.matmul(pre[h][:], wd_sb[:, k, :], diff_bf[:, cols], start=first, stop=False)
+                nc.tensor.matmul(pre[h][:], wp_sb[:, k, :], prod_bf[:, cols], start=first, stop=False)
             for h, cols in enumerate(HALVES):
-                nc.tensor.matmul(pre[h][:], wp_sb[:, k, :], prod_bf[:, cols], start=False, stop=last)
+                nc.tensor.matmul(pre[h][:], wd_sb[:, k, :], diff_bf[:, cols], start=False, stop=last)
 
         for h, cols in enumerate(HALVES):
             gate = held.tile([M, N // 2], F32, name=f"gate{h}")

@@ -50,9 +50,8 @@ def tile_edgegate_kernel(tc, x, hv, wd, wp, ws, wf, b1, se, fe, offs, out):
             nc.sync.dma_start(x_blk[:], x_by_block[k])
             x_blocks.append(x_blk)
             hv_blocks.append(hv_blk)
-            if k == 1:
-                nc.sync.dma_start(wd_sb[:], wd.rearrange("(p k) m -> p k m", k=BLOCKS))
-                nc.sync.dma_start(wp_sb[:], wp.rearrange("(p k) m -> p k m", k=BLOCKS))
+        nc.sync.dma_start(wd_sb[:], wd.rearrange("(p k) m -> p k m", k=BLOCKS))
+        nc.sync.dma_start(wp_sb[:], wp.rearrange("(p k) m -> p k m", k=BLOCKS))
 
         pre = [psum.tile([M, N // 2], F32, name=f"pre{h}") for h in range(len(HALVES))]
 
@@ -77,11 +76,11 @@ def tile_edgegate_kernel(tc, x, hv, wd, wp, ws, wf, b1, se, fe, offs, out):
             else:
                 nc.scalar.activation(diff_bf[:], signed_diff[:], ACT.Abs)
 
-            if k == BLOCKS // 2:
+            if first:
                 for h, cols in enumerate(HALVES):
-                    nc.tensor.matmul(pre[h][:], edge_weights[:], edge_features[:, cols], start=False, stop=False)
+                    nc.tensor.matmul(pre[h][:], edge_weights[:], edge_features[:, cols], start=True, stop=False)
             for h, cols in enumerate(HALVES):
-                nc.tensor.matmul(pre[h][:], wp_sb[:, k, :], prod_bf[:, cols], start=first, stop=False)
+                nc.tensor.matmul(pre[h][:], wp_sb[:, k, :], prod_bf[:, cols], start=False, stop=False)
             for h, cols in enumerate(HALVES):
                 nc.tensor.matmul(pre[h][:], wd_sb[:, k, :], diff_bf[:, cols], start=False, stop=last)
 

@@ -65,7 +65,12 @@ def tile_edgegate_kernel(tc, x, hv, wd, wp, ws, wf, b1, se, fe, offs, out):
             prod = blocks.tile([P, N], F32, name="prod")
             nc.vector.tensor_tensor(prod[:], looked_up, hv_blocks[k][:], ALU.mult)
             signed_diff = blocks.tile([P, N], F32, name="signed_diff")
-            nc.vector.tensor_tensor(signed_diff[:], looked_up, neg_hv[:], ALU.add)
+            if last:
+                for cols in HALVES:
+                    half_looked_up = x_blocks[k][:].indirect(offsets[:, cols.start // 16 : cols.stop // 16])
+                    nc.vector.tensor_tensor(signed_diff[:, cols], half_looked_up, neg_hv[:, cols], ALU.add)
+            else:
+                nc.vector.tensor_tensor(signed_diff[:], looked_up, neg_hv[:], ALU.add)
 
             prod_bf = blocks.tile([P, N], BF16, name="prod_bf")
             nc.scalar.activation(prod_bf[:], prod[:], ACT.Copy)

@@ -44,12 +44,13 @@ def tile_edgegate_kernel(tc, x, hv, wd, wp, ws, wf, b1, se, fe, offs, out):
         x_blocks = []
         hv_blocks = []
         for k in range(BLOCKS):
-            x_blk = blocks.tile([P, S], F32, name="x_blk")
-            hv_blk = blocks.tile([P, N], F32, name="hv_blk")
-            nc.sync.dma_start(hv_blk[:], hv_by_block[k])
-            nc.sync.dma_start(x_blk[:], x_by_block[k])
-            x_blocks.append(x_blk)
-            hv_blocks.append(hv_blk)
+            x_blocks.append(blocks.tile([P, S], F32, name="x_blk"))
+            hv_blocks.append(blocks.tile([P, N], F32, name="hv_blk"))
+        nc.sync.dma_start(hv_blocks[0][:], hv_by_block[0])
+        for k in range(BLOCKS):
+            nc.sync.dma_start(x_blocks[k][:], x_by_block[k])
+            if k + 1 < BLOCKS:
+                nc.sync.dma_start(hv_blocks[k + 1][:], hv_by_block[k + 1])
         nc.sync.dma_start(wd_sb[:], wd.rearrange("(p k) m -> p k m", k=BLOCKS))
         nc.sync.dma_start(wp_sb[:], wp.rearrange("(p k) m -> p k m", k=BLOCKS))
 
@@ -63,31 +64,33 @@ def tile_edgegate_kernel(tc, x, hv, wd, wp, ws, wf, b1, se, fe, offs, out):
             nc.scalar.activation(neg_hv[:], hv_blocks[k][:], ACT.Copy, scale=-1.0)
 
             prod = blocks.tile([P, N], F32, name="prod")
-            nc.vector.tensor_tensor(prod[:], looked_up, hv_blocks[k][:], ALU.mult)
-            signed_diff = blocks.tile([P, N], F32, name="signed_diff")
-            if last:
-                for cols in HALVES:
-                    half_looked_up = x_blocks[k][:].indirect(offsets[:, cols.start // 16 : cols.stop // 16])
-                    nc.vector.tensor_tensor(signed_diff[:, cols], half_looked_up, neg_hv[:, cols], ALU.add)
-            else:
-                nc.vector.tensor_tensor(signed_diff[:], looked_up, neg_hv[:], ALU.add)
-
             prod_bf = blocks.tile([P, N], BF16, name="prod_bf")
-            nc.scalar.activation(prod_bf[:], prod[:], ACT.Copy)
+            signed_diff = blocks.tile([P, N], F32, name="signed_diff")
             diff_bf = blocks.tile([P, N], BF16, name="diff_bf")
             if last:
+                nc.vector.tensor_tensor(signed_diff[:], looked_up, neg_hv[:], ALU.add)
+                nc.scalar.activation(diff_bf[:], signed_diff[:], ACT.Abs)
                 for cols in HALVES:
-                    nc.scalar.activation(diff_bf[:, cols], signed_diff[:, cols], ACT.Abs)
+                    half_looked_up = x_blocks[k][:].indirect(offsets[:, cols.start // 16 : cols.stop // 16])
+                    nc.vector.tensor_tensor(prod[:, cols], half_looked_up, hv_blocks[k][:, cols], ALU.mult)
+                nc.scalar.activation(prod_bf[:, HALVES[0]], prod[:, HALVES[0]], ACT.Copy)
+                nc.vector.tensor_copy(prod_bf[:, HALVES[1]], prod[:, HALVES[1]])
             else:
+                nc.vector.tensor_tensor(prod[:], looked_up, hv_blocks[k][:], ALU.mult)
+                nc.vector.tensor_tensor(signed_diff[:], looked_up, neg_hv[:], ALU.add)
+                nc.scalar.activation(prod_bf[:], prod[:], ACT.Copy)
                 nc.scalar.activation(diff_bf[:], signed_diff[:], ACT.Abs)
 
             if first:
                 for h, cols in enumerate(HALVES):
                     nc.tensor.matmul(pre[h][:], edge_weights[:], edge_features[:, cols], start=True, stop=False)
-            for h, cols in enumerate(HALVES):
-                nc.tensor.matmul(pre[h][:], wp_sb[:, k, :], prod_bf[:, cols], start=False, stop=False)
-            for h, cols in enumerate(HALVES):
-                nc.tensor.matmul(pre[h][:], wd_sb[:, k, :], diff_bf[:, cols], start=False, stop=last)
+            terms = [(wp_sb, prod_bf), (wd_sb, diff_bf)]
+            if last:
+                terms = terms[::-1]
+            for i, (weights, values) in enumerate(terms):
+                for h, cols in enumerate(HALVES):
+                    closes = last and i == len(terms) - 1
+                    nc.tensor.matmul(pre[h][:], weights[:, k, :], values[:, cols], start=False, stop=closes)
 
         for h, cols in enumerate(HALVES):
             gate = held.tile([M, N // 2], F32, name=f"gate{h}")

@@ -95,5 +95,4 @@ def tile_edgegate_kernel(tc, x, hv, wd, wp, ws, wf, b1, se, fe, offs, out):
         for h, cols in enumerate(HALVES):
             gate = held.tile([M, N // 2], F32, name=f"gate{h}")
             nc.scalar.activation(gate[:], pre[h][:], ACT.Silu)
-            queue = nc.sync if h == 0 else nc.scalar
-            queue.dma_start(out[:, cols], gate[:])
+            nc.sync.dma_start(out[:, cols], gate[:])

@@ -11,6 +11,7 @@ C, S, N, M = 1024, 1024, 512, 128
 BLOCKS = C // P
 EDGE_ROWS = 3
 HALVES = (slice(0, N // 2), slice(N // 2, N))
+LAST_PIECES = (slice(0, N // 2), slice(N // 2, 3 * N // 4), slice(3 * N // 4, N))
 
 FLOPS = 2 * (2 * C + EDGE_ROWS) * M * N
 
@@ -70,11 +71,12 @@ def tile_edgegate_kernel(tc, x, hv, wd, wp, ws, wf, b1, se, fe, offs, out):
             if last:
                 nc.vector.tensor_tensor(signed_diff[:], looked_up, neg_hv[:], ALU.add)
                 nc.scalar.activation(diff_bf[:], signed_diff[:], ACT.Abs)
-                for cols in HALVES:
-                    half_looked_up = x_blocks[k][:].indirect(offsets[:, cols.start // 16 : cols.stop // 16])
-                    nc.vector.tensor_tensor(prod[:, cols], half_looked_up, hv_blocks[k][:, cols], ALU.mult)
-                nc.scalar.activation(prod_bf[:, HALVES[0]], prod[:, HALVES[0]], ACT.Copy)
-                nc.vector.tensor_copy(prod_bf[:, HALVES[1]], prod[:, HALVES[1]])
+                for cols in LAST_PIECES:
+                    piece_looked_up = x_blocks[k][:].indirect(offsets[:, cols.start // 16 : cols.stop // 16])
+                    nc.vector.tensor_tensor(prod[:, cols], piece_looked_up, hv_blocks[k][:, cols], ALU.mult)
+                for cols in LAST_PIECES[:-1]:
+                    nc.scalar.activation(prod_bf[:, cols], prod[:, cols], ACT.Copy)
+                nc.vector.tensor_copy(prod_bf[:, LAST_PIECES[-1]], prod[:, LAST_PIECES[-1]])
             else:
                 nc.vector.tensor_tensor(prod[:], looked_up, hv_blocks[k][:], ALU.mult)
                 nc.vector.tensor_tensor(signed_diff[:], looked_up, neg_hv[:], ALU.add)
@@ -84,13 +86,13 @@ def tile_edgegate_kernel(tc, x, hv, wd, wp, ws, wf, b1, se, fe, offs, out):
             if first:
                 for h, cols in enumerate(HALVES):
                     nc.tensor.matmul(pre[h][:], edge_weights[:], edge_features[:, cols], start=True, stop=False)
-            terms = [(wp_sb, prod_bf), (wd_sb, diff_bf)]
-            if last:
-                terms = terms[::-1]
-            for i, (weights, values) in enumerate(terms):
-                for h, cols in enumerate(HALVES):
-                    closes = last and i == len(terms) - 1
-                    nc.tensor.matmul(pre[h][:], weights[:, k, :], values[:, cols], start=False, stop=closes)
+            for h, cols in enumerate(HALVES):
+                nc.tensor.matmul(pre[h][:], wd_sb[:, k, :], diff_bf[:, cols], start=False, stop=False)
+            for cols in LAST_PIECES if last else HALVES:
+                h = cols.start // (N // 2)
+                part = pre[h][:, cols.start - h * N // 2 : cols.stop - h * N // 2]
+                closes = last and cols.stop == HALVES[h].stop
+                nc.tensor.matmul(part, wp_sb[:, k, :], prod_bf[:, cols], start=False, stop=closes)
 
         for h, cols in enumerate(HALVES):
             gate = held.tile([M, N // 2], F32, name=f"gate{h}")

@@ -47,11 +47,13 @@ def tile_edgegate_kernel(tc, x, hv, wd, wp, ws, wf, b1, se, fe, offs, out):
         for k in range(BLOCKS):
             x_blocks.append(blocks.tile([P, S], F32, name="x_blk"))
             hv_blocks.append(blocks.tile([P, N], F32, name="hv_blk"))
-        nc.sync.dma_start(hv_blocks[0][:], hv_by_block[0])
+        nc.sync.dma_start(hv_blocks[0][:, HALVES[0]], hv_by_block[0][:, HALVES[0]])
         for k in range(BLOCKS):
             nc.sync.dma_start(x_blocks[k][:], x_by_block[k])
             if k + 1 < BLOCKS:
                 nc.sync.dma_start(hv_blocks[k + 1][:], hv_by_block[k + 1])
+            if k == 0:
+                nc.sync.dma_start(hv_blocks[0][:, HALVES[1]], hv_by_block[0][:, HALVES[1]])
         nc.sync.dma_start(wd_sb[:], wd.rearrange("(p k) m -> p k m", k=BLOCKS))
         nc.sync.dma_start(wp_sb[:], wp.rearrange("(p k) m -> p k m", k=BLOCKS))
 
@@ -60,9 +62,11 @@ def tile_edgegate_kernel(tc, x, hv, wd, wp, ws, wf, b1, se, fe, offs, out):
         for k in range(BLOCKS):
             first, last = k == 0, k == BLOCKS - 1
             looked_up = x_blocks[k][:].indirect(offsets[:])
+            pieces = HALVES if first else (slice(0, N),)
 
             neg_hv = blocks.tile([P, N], F32, name="neg_hv")
-            nc.scalar.activation(neg_hv[:], hv_blocks[k][:], ACT.Copy, scale=-1.0)
+            for cols in pieces:
+                nc.scalar.activation(neg_hv[:, cols], hv_blocks[k][:, cols], ACT.Copy, scale=-1.0)
 
             prod = blocks.tile([P, N], F32, name="prod")
             prod_bf = blocks.tile([P, N], BF16, name="prod_bf")
@@ -78,8 +82,10 @@ def tile_edgegate_kernel(tc, x, hv, wd, wp, ws, wf, b1, se, fe, offs, out):
                     nc.scalar.activation(prod_bf[:, cols], prod[:, cols], ACT.Copy)
                 nc.vector.tensor_copy(prod_bf[:, LAST_PIECES[-1]], prod[:, LAST_PIECES[-1]])
             else:
-                nc.vector.tensor_tensor(prod[:], looked_up, hv_blocks[k][:], ALU.mult)
-                nc.vector.tensor_tensor(signed_diff[:], looked_up, neg_hv[:], ALU.add)
+                for cols in pieces:
+                    piece_looked_up = x_blocks[k][:].indirect(offsets[:, cols.start // 16 : cols.stop // 16])
+                    nc.vector.tensor_tensor(prod[:, cols], piece_looked_up, hv_blocks[k][:, cols], ALU.mult)
+                    nc.vector.tensor_tensor(signed_diff[:, cols], piece_looked_up, neg_hv[:, cols], ALU.add)
                 nc.scalar.activation(prod_bf[:], prod[:], ACT.Copy)
                 nc.scalar.activation(diff_bf[:], signed_diff[:], ACT.Abs)
 

import concourse.mybir as mybir

F32 = mybir.dt.float32
BF16 = mybir.dt.bfloat16
U16 = mybir.dt.uint16
ACT = mybir.ActivationFunctionType
ALU = mybir.AluOpType

P = 128
C, S, N, M = 1024, 1024, 512, 128
BLOCKS = C // P
EDGE_ROWS = 3
HALVES = (slice(0, N // 2), slice(N // 2, N))
LAST_PIECES = (slice(0, N // 2), slice(N // 2, 3 * N // 4), slice(3 * N // 4, N))

FLOPS = 2 * (2 * C + EDGE_ROWS) * M * N


def tile_edgegate_kernel(tc, x, hv, wd, wp, ws, wf, b1, se, fe, offs, out):
    nc = tc.nc
    with (
        tc.tile_pool(name="held", bufs=1) as held,
        tc.tile_pool(name="blocks", bufs=BLOCKS) as blocks,
        tc.psum_pool(name="psum", bufs=1) as psum,
    ):
        offsets = held.tile([P, N // 16], U16, name="offsets")
        nc.sync.dma_start(offsets[:], offs)

        edge_weights = held.tile([EDGE_ROWS, M], F32, name="edge_weights")
        edge_features = held.tile([EDGE_ROWS, N], F32, name="edge_features")
        nc.vector.memset(edge_features[0:1, :], 1.0)
        nc.gpsimd.dma_start(edge_weights[0:1, :], b1.rearrange("m o -> o m"))
        nc.gpsimd.dma_start(edge_weights[1:2, :], ws.rearrange("m o -> o m"))
        nc.gpsimd.dma_start(edge_weights[2:3, :], wf.rearrange("m o -> o m"))
        nc.gpsimd.dma_start(edge_features[1:2, :], se)
        nc.gpsimd.dma_start(edge_features[2:3, :], fe)

        warm = held.tile([1, 1], F32, name="warm")
        nc.scalar.activation(warm[:], edge_features[0:1, 0:1], ACT.Silu)

        x_by_block = x.rearrange("(p k) s -> k p s", k=BLOCKS)
        hv_by_block = hv.rearrange("(p k) n -> k p n", k=BLOCKS)
        wd_sb = held.tile([P, BLOCKS, M], BF16, name="wd_sb")
        wp_sb = held.tile([P, BLOCKS, M], BF16, name="wp_sb")
        x_blocks = []
        hv_blocks = []
        for k in range(BLOCKS):
            x_blocks.append(blocks.tile([P, S], F32, name="x_blk"))
            hv_blocks.append(blocks.tile([P, N], F32, name="hv_blk"))
        nc.sync.dma_start(hv_blocks[0][:, HALVES[0]], hv_by_block[0][:, HALVES[0]])
        for k in range(BLOCKS):
            nc.sync.dma_start(x_blocks[k][:], x_by_block[k])
            if k + 1 < BLOCKS:
                nc.sync.dma_start(hv_blocks[k + 1][:], hv_by_block[k + 1])
            if k == 0:
                nc.sync.dma_start(hv_blocks[0][:, HALVES[1]], hv_by_block[0][:, HALVES[1]])
        nc.sync.dma_start(wd_sb[:], wd.rearrange("(p k) m -> p k m", k=BLOCKS))
        nc.sync.dma_start(wp_sb[:], wp.rearrange("(p k) m -> p k m", k=BLOCKS))

        pre = [psum.tile([M, N // 2], F32, name=f"pre{h}") for h in range(len(HALVES))]

        for k in range(BLOCKS):
            first, last = k == 0, k == BLOCKS - 1
            looked_up = x_blocks[k][:].indirect(offsets[:])
            pieces = HALVES if first else (slice(0, N),)

            neg_hv = blocks.tile([P, N], F32, name="neg_hv")
            for cols in pieces:
                nc.scalar.activation(neg_hv[:, cols], hv_blocks[k][:, cols], ACT.Copy, scale=-1.0)

            prod = blocks.tile([P, N], F32, name="prod")
            prod_bf = blocks.tile([P, N], BF16, name="prod_bf")
            signed_diff = blocks.tile([P, N], F32, name="signed_diff")
            diff_bf = blocks.tile([P, N], BF16, name="diff_bf")
            if last:
                nc.vector.tensor_tensor(signed_diff[:], looked_up, neg_hv[:], ALU.add)
                nc.scalar.activation(diff_bf[:], signed_diff[:], ACT.Abs)
                for cols in LAST_PIECES:
                    piece_looked_up = x_blocks[k][:].indirect(offsets[:, cols.start // 16 : cols.stop // 16])
                    nc.vector.tensor_tensor(prod[:, cols], piece_looked_up, hv_blocks[k][:, cols], ALU.mult)
                for cols in LAST_PIECES[:-1]:
                    nc.scalar.activation(prod_bf[:, cols], prod[:, cols], ACT.Copy)
                nc.vector.tensor_copy(prod_bf[:, LAST_PIECES[-1]], prod[:, LAST_PIECES[-1]])
            else:
                for cols in pieces:
                    piece_looked_up = x_blocks[k][:].indirect(offsets[:, cols.start // 16 : cols.stop // 16])
                    nc.vector.tensor_tensor(prod[:, cols], piece_looked_up, hv_blocks[k][:, cols], ALU.mult)
                    nc.vector.tensor_tensor(signed_diff[:, cols], piece_looked_up, neg_hv[:, cols], ALU.add)
                nc.scalar.activation(prod_bf[:], prod[:], ACT.Copy)
                nc.scalar.activation(diff_bf[:], signed_diff[:], ACT.Abs)

            if first:
                for h, cols in enumerate(HALVES):
                    nc.tensor.matmul(pre[h][:], edge_weights[:], edge_features[:, cols], start=True, stop=False)
            for h, cols in enumerate(HALVES):
                nc.tensor.matmul(pre[h][:], wd_sb[:, k, :], diff_bf[:, cols], start=False, stop=False)
            for cols in LAST_PIECES if last else HALVES:
                h = cols.start // (N // 2)
                part = pre[h][:, cols.start - h * N // 2 : cols.stop - h * N // 2]
                closes = last and cols.stop == HALVES[h].stop
                nc.tensor.matmul(part, wp_sb[:, k, :], prod_bf[:, cols], start=False, stop=closes)

        for h, cols in enumerate(HALVES):
            gate = held.tile([M, N // 2], F32, name=f"gate{h}")
            nc.scalar.activation(gate[:], pre[h][:], ACT.Silu)
            nc.sync.dma_start(out[:, cols], gate[:])
